import numpy as np
import ml_dtypes


def mxq(x, axis, fmt="e4m3"):
    dtype, down = {"e4m3": (ml_dtypes.float8_e4m3fn, 7), "e5m2": (ml_dtypes.float8_e5m2, 14)}[fmt]
    v = np.moveaxis(np.asarray(x, np.float32).astype(ml_dtypes.bfloat16).astype(np.float64), axis, -1)
    blocks = v.reshape(v.shape[:-1] + (-1, 32))
    amax = np.abs(blocks).max(-1, keepdims=True)
    byte = np.maximum(np.where(amax > 0, np.frexp(amax)[1] - 1 + 127, 0) - down, 1)
    scale = np.exp2(byte - 127.0)
    codes = (blocks / scale).astype(np.float32).astype(dtype).astype(np.float64)
    return np.moveaxis((codes * scale).reshape(v.shape), -1, axis)


WIDE = False


def mx_kscale(k):
    if not WIDE:
        return np.ones(k)
    levels = np.array([10, -10, 5, -5, 0])
    if k % 512:
        return np.exp2(np.random.permutation(np.resize(levels, k // 32))).repeat(32)
    a = np.empty((k // 512, 16))
    for p in range(k // 512):
        a[p, :8] = np.random.permutation(np.resize(levels, 8))
        for g in range(8):
            far = levels[np.abs(levels - a[p, g]) >= 10]
            a[p, g + 8] = far[np.random.randint(len(far))]
    return np.exp2(a.ravel()).repeat(32)


BF16 = ml_dtypes.bfloat16


def bf(x):
    return np.asarray(x, np.float32).astype(BF16)


def f64(x):
    return np.asarray(x).astype(np.float64)


NS, NI, T = 1024, 512, 1025
NA = NS + NI


def setup_inputs():
    s = mx_kscale(NA)
    r = s[:NS]
    A = np.random.standard_normal((NS, NS)) / np.sqrt(NA)
    B = np.random.standard_normal((NS, NI)) / np.sqrt(NA)
    x0 = np.random.standard_normal(NS) * 3.0
    V = np.random.standard_normal((T, NA))
    V[0, :NS] *= 3.0
    return {"A": bf(A * r[:, None] / s[None, :NS]), "B": bf(B * r[:, None] / s[None, NS:]), "x0": bf(x0 * r),
            "net_input": bf((V * s[None, :]).reshape(-1)), "T": T}


def reference(A, B, x0, net_input, T):
    n_state = A.shape[0]
    n_all = n_state + B.shape[1]
    AB = np.concatenate([f64(A), f64(B)], axis=1)
    V = f64(net_input).reshape(T, n_all)
    out0 = V[0, :n_state] - f64(x0)
    prop = mxq(V[:-1], 1, "e4m3") @ mxq(AB, 1, "e4m3").T
    out_rest = prop - V[1:, :n_state]
    return np.concatenate([out0, out_rest.reshape(-1)])

@@ -1,0 +1,165 @@
+from contextlib import ExitStack
+
+import concourse.mybir as mybir
+from concourse.masks import make_identity
+
+F32 = mybir.dt.float32
+BF16 = mybir.dt.bfloat16
+U32 = mybir.dt.uint32
+U8 = mybir.dt.uint8
+FP8X4 = mybir.dt.float8_e4m3fn_x4
+
+P = 128
+N_STATE = 1024
+N_ALL = 1536
+STEPS = 1024
+PASSES = 3
+WORDS = 2
+SLOTS = STEPS // P
+TILES = N_STATE // P
+PAIR = 2 * P
+N_HALF = 512
+HALVES = N_STATE // N_HALF
+FIRST_P = 16
+WARM_UP = 4
+
+FLOPS = 2 * STEPS * N_STATE * N_ALL
+
+
+def prepare_pair(nc, banks, ident, raw, pair, grouped, codes, scales, hold_clock):
+    cols = slice(pair * PAIR, (pair + 1) * PAIR)
+    for g in range(PASSES):
+        bank = banks.tile([P, WORDS, PAIR], F32)
+        for t in range(2):
+            row_words = raw[:, 2 * pair + t, :].bitcast(F32)
+            for u in range(WORDS):
+                words = slice(WORDS * P * g + u, WORDS * P * (g + 1), WORDS)
+                nc.tensor.transpose(
+                    bank[:, u, t * P : (t + 1) * P], row_words[:, words], ident[:]
+                )
+        hold_clock()
+        nc.scalar.copy(out=grouped[:, g, cols, :], in_=bank[:].rearrange("p u r -> p r u"))
+    for g in range(PASSES):
+        nc.vector.quantize_mx(
+            out=codes[:, g, cols].bitcast(FP8X4),
+            scales=scales[:, g, cols],
+            in_=grouped[:, g, cols, :].rearrange("p r u -> p (r u)").bitcast(BF16),
+        )
+
+
+def tile_constrainnet_kernel(tc, A, B, x0, net_input, T, out):
+    nc = tc.nc
+    assert T == STEPS + 1
+
+    v_rows = net_input[0 : STEPS * N_ALL].rearrange("(p s k) -> p s k", s=SLOTS, k=N_ALL)
+    v_next = net_input[N_ALL : (STEPS + 1) * N_ALL].rearrange("(p s k) -> p s k", s=SLOTS, k=N_ALL)
+    r_next = out[N_STATE : (STEPS + 1) * N_STATE].rearrange("(p s i) -> p s i", s=SLOTS, i=N_STATE)
+    a_rows = A.rearrange("(m p) k -> p m k", p=P)
+    b_rows = B.rearrange("(m p) k -> p m k", p=P)
+
+    with ExitStack() as ctx:
+        keep = ctx.enter_context(tc.tile_pool(name="keep", bufs=1))
+        banks = ctx.enter_context(tc.psum_pool(name="banks", bufs=4))
+        sums = ctx.enter_context(tc.psum_pool(name="sums", bufs=4))
+
+        ident = keep.tile([P, P], F32)
+        make_identity(nc, ident[:])
+
+        ab_raw = keep.tile([P, TILES, N_ALL], BF16)
+        v_raw = keep.tile([P, SLOTS + 1, N_ALL], BF16)
+        ab_grouped = keep.tile([P, PASSES, N_STATE, WORDS], F32, align_bytes=64)
+        v_grouped = keep.tile([P, PASSES, STEPS, WORDS], F32, align_bytes=64)
+        ab_codes = keep.tile([P, PASSES, N_STATE], U32, align_bytes=64)
+        ab_scales = keep.tile([P, PASSES, N_STATE], U8, align_bytes=64)
+        v_codes = keep.tile([P, PASSES, STEPS], U32, align_bytes=64)
+        v_scales = keep.tile([P, PASSES, STEPS], U8, align_bytes=64)
+        r_sb = keep.tile([P, SLOTS, N_STATE], F32)
+        x_first = keep.tile([FIRST_P, N_STATE // FIRST_P], BF16)
+        x_given = keep.tile([FIRST_P, N_STATE // FIRST_P], BF16)
+        r_first = keep.tile([FIRST_P, N_STATE // FIRST_P], F32)
+
+        def load_ab(pair):
+            tiles = slice(2 * pair, 2 * pair + 2)
+            nc.sync.dma_start(out=ab_raw[:, tiles, 0:N_STATE], in_=a_rows[:, tiles, :])
+            nc.sync.dma_start(out=ab_raw[:, tiles, N_STATE:N_ALL], in_=b_rows[:, tiles, :])
+
+        def load_v(pair):
+            slots = slice(2 * pair, 2 * pair + 2)
+            nc.sync.dma_start(out=v_raw[:, slots, :], in_=v_rows[:, slots, :])
+
+        zeros = keep.tile([P, N_HALF], BF16)
+        nc.vector.memset(zeros[:], 0.0)
+
+        def matmul_of_zeros():
+            unread = sums.tile([P, N_HALF], F32, tag="acc")
+            nc.tensor.matmul(out=unread[:], lhsT=zeros[:, 0:P], rhs=zeros[:], start=True, stop=True)
+
+        def nothing():
+            return None
+
+        def prepare_ab(pair, hold_clock):
+            prepare_pair(nc, banks, ident, ab_raw, pair, ab_grouped, ab_codes, ab_scales, hold_clock)
+
+        def prepare_v(pair, hold_clock):
+            prepare_pair(nc, banks, ident, v_raw, pair, v_grouped, v_codes, v_scales, hold_clock)
+
+        def multiply(pair, h):
+            n_cols = slice(h * N_HALF, (h + 1) * N_HALF)
+            for s in range(2 * pair, 2 * pair + 2):
+                m_cols = slice(s * P, (s + 1) * P)
+                acc = sums.tile([P, N_HALF], F32)
+                for g in range(PASSES):
+                    nc.tensor.matmul_mx(
+                        out=acc[:],
+                        lhsT=v_codes[:, g, m_cols].bitcast(FP8X4),
+                        lhsT_scale=v_scales[:, g, m_cols],
+                        rhs=ab_codes[:, g, n_cols].bitcast(FP8X4),
+                        rhs_scale=ab_scales[:, g, n_cols],
+                        start=(g == 0),
+                        stop=(g == PASSES - 1),
+                    )
+                nc.vector.tensor_tensor(
+                    out=r_sb[:, s, n_cols],
+                    in0=acc[:],
+                    in1=v_raw[:, s + 1, n_cols],
+                    op=mybir.AluOpType.subtract,
+                )
+                nc.sync.dma_start(out=r_next[:, s, n_cols], in_=r_sb[:, s, n_cols])
+
+        with tc.manual_schedule():
+            nc.scalar.dma_start(
+                out=x_first[:], in_=net_input[0:N_STATE].rearrange("(p c) -> p c", p=FIRST_P)
+            )
+            nc.scalar.dma_start(out=x_given[:], in_=x0.rearrange("(p c) -> p c", p=FIRST_P))
+            load_ab(0)
+            load_ab(1)
+            for pair in range(SLOTS // 2):
+                load_v(pair)
+            nc.sync.dma_start(out=v_raw[:, SLOTS, 0:N_STATE], in_=v_next[:, SLOTS - 1, 0:N_STATE])
+            load_ab(2)
+            load_ab(3)
+
+            for i in range(WARM_UP):
+                matmul_of_zeros()
+            prepare_ab(0, matmul_of_zeros)
+            prepare_ab(1, matmul_of_zeros)
+
+            nc.vector.tensor_tensor(
+                out=r_first[:], in0=x_first[:], in1=x_given[:], op=mybir.AluOpType.subtract
+            )
+            nc.sync.dma_start(
+                out=out[0:N_STATE].rearrange("(p c) -> p c", p=FIRST_P), in_=r_first[:]
+            )
+
+            prepare_v(0, matmul_of_zeros)
+            prepare_v(1, matmul_of_zeros)
+            multiply(0, 0)
+            for pair in range(1, SLOTS // 2):
+                if pair + 1 < SLOTS // 2:
+                    prepare_v(pair + 1, nothing)
+                else:
+                    prepare_ab(2, nothing)
+                    prepare_ab(3, nothing)
+                multiply(pair, 0)
+            for pair in range(SLOTS // 2):
+                multiply(pair, 1)

@@ -26,17 +26,27 @@ WARM_UP = 4
 FLOPS = 2 * STEPS * N_STATE * N_ALL
 
 
-def prepare_pair(nc, banks, ident, raw, pair, grouped, codes, scales, hold_clock):
+def split_words(nc, raw, pair, split):
+    for t in (2 * pair, 2 * pair + 1):
+        nc.vector.tensor_copy(
+            out=split[:, t, :].rearrange("p (g u w) -> p g u w", u=WORDS, w=P),
+            in_=raw[:, t, :].bitcast(F32).rearrange("p (g w u) -> p g u w", u=WORDS, w=P),
+        )
+
+
+def prepare_pair(nc, banks, ident, raw, split, pair, grouped, codes, scales, hold_clock):
     cols = slice(pair * PAIR, (pair + 1) * PAIR)
     for g in range(PASSES):
         bank = banks.tile([P, WORDS, PAIR], F32)
         for t in range(2):
-            row_words = raw[:, 2 * pair + t, :].bitcast(F32)
             for u in range(WORDS):
-                words = slice(WORDS * P * g + u, WORDS * P * (g + 1), WORDS)
-                nc.tensor.transpose(
-                    bank[:, u, t * P : (t + 1) * P], row_words[:, words], ident[:]
-                )
+                if split is None:
+                    every_second = slice(WORDS * P * g + u, WORDS * P * (g + 1), WORDS)
+                    words = raw[:, 2 * pair + t, :].bitcast(F32)[:, every_second]
+                else:
+                    first = (WORDS * g + u) * P
+                    words = split[:, 2 * pair + t, first : first + P]
+                nc.tensor.transpose(bank[:, u, t * P : (t + 1) * P], words, ident[:])
         hold_clock()
         nc.scalar.copy(out=grouped[:, g, cols, :], in_=bank[:].rearrange("p u r -> p r u"))
     for g in range(PASSES):
@@ -67,6 +77,8 @@ def tile_constrainnet_kernel(tc, A, B, x0, net_input, T, out):
 
         ab_raw = keep.tile([P, TILES, N_ALL], BF16)
         v_raw = keep.tile([P, SLOTS + 1, N_ALL], BF16)
+        ab_split = keep.tile([P, TILES, N_ALL // 2], F32)
+        v_split = keep.tile([P, SLOTS, N_ALL // 2], F32)
         ab_grouped = keep.tile([P, PASSES, N_STATE, WORDS], F32, align_bytes=64)
         v_grouped = keep.tile([P, PASSES, STEPS, WORDS], F32, align_bytes=64)
         ab_codes = keep.tile([P, PASSES, N_STATE], U32, align_bytes=64)
@@ -97,11 +109,13 @@ def tile_constrainnet_kernel(tc, A, B, x0, net_input, T, out):
         def nothing():
             return None
 
-        def prepare_ab(pair, hold_clock):
-            prepare_pair(nc, banks, ident, ab_raw, pair, ab_grouped, ab_codes, ab_scales, hold_clock)
+        def prepare_ab(pair, split, hold_clock):
+            prepare_pair(
+                nc, banks, ident, ab_raw, split, pair, ab_grouped, ab_codes, ab_scales, hold_clock
+            )
 
-        def prepare_v(pair, hold_clock):
-            prepare_pair(nc, banks, ident, v_raw, pair, v_grouped, v_codes, v_scales, hold_clock)
+        def prepare_v(pair, split, hold_clock):
+            prepare_pair(nc, banks, ident, v_raw, split, pair, v_grouped, v_codes, v_scales, hold_clock)
 
         def multiply(pair, h):
             n_cols = slice(h * N_HALF, (h + 1) * N_HALF)
@@ -141,8 +155,8 @@ def tile_constrainnet_kernel(tc, A, B, x0, net_input, T, out):
 
             for i in range(WARM_UP):
                 matmul_of_zeros()
-            prepare_ab(0, matmul_of_zeros)
-            prepare_ab(1, matmul_of_zeros)
+            prepare_ab(0, None, matmul_of_zeros)
+            prepare_ab(1, None, matmul_of_zeros)
 
             nc.vector.tensor_tensor(
                 out=r_first[:], in0=x_first[:], in1=x_given[:], op=mybir.AluOpType.subtract
@@ -151,15 +165,19 @@ def tile_constrainnet_kernel(tc, A, B, x0, net_input, T, out):
                 out=out[0:N_STATE].rearrange("(p c) -> p c", p=FIRST_P), in_=r_first[:]
             )
 
-            prepare_v(0, matmul_of_zeros)
-            prepare_v(1, matmul_of_zeros)
+            prepare_v(0, None, matmul_of_zeros)
+            prepare_v(1, None, matmul_of_zeros)
+            split_words(nc, v_raw, 2, v_split)
             multiply(0, 0)
-            for pair in range(1, SLOTS // 2):
-                if pair + 1 < SLOTS // 2:
-                    prepare_v(pair + 1, nothing)
-                else:
-                    prepare_ab(2, nothing)
-                    prepare_ab(3, nothing)
-                multiply(pair, 0)
+            prepare_v(2, v_split, nothing)
+            split_words(nc, v_raw, 3, v_split)
+            multiply(1, 0)
+            prepare_v(3, v_split, nothing)
+            split_words(nc, ab_raw, 2, ab_split)
+            split_words(nc, ab_raw, 3, ab_split)
+            multiply(2, 0)
+            prepare_ab(2, ab_split, nothing)
+            prepare_ab(3, ab_split, nothing)
+            multiply(3, 0)
             for pair in range(SLOTS // 2):
                 multiply(pair, 1)

@@ -26,29 +26,35 @@ WARM_UP = 4
 FLOPS = 2 * STEPS * N_STATE * N_ALL
 
 
-def split_words(nc, raw, pair, split):
+def split_words(nc, operand, pair):
+    raw, split = operand[0], operand[1]
     for t in (2 * pair, 2 * pair + 1):
         nc.vector.tensor_copy(
-            out=split[:, t, :].rearrange("p (g u w) -> p g u w", u=WORDS, w=P),
-            in_=raw[:, t, :].bitcast(F32).rearrange("p (g w u) -> p g u w", u=WORDS, w=P),
+            out=split[:, t, :].rearrange("p (g u w) -> p u g w", u=WORDS, w=P),
+            in_=raw[:, t, 0:N_ALL].bitcast(F32).rearrange("p (g w u) -> p u g w", u=WORDS, w=P),
         )
 
 
-def prepare_pair(nc, banks, ident, raw, split, pair, grouped, codes, scales, hold_clock):
+def transpose_pair(nc, banks, ident, operand, pair, hold_clock):
+    split, grouped = operand[1], operand[2]
     cols = slice(pair * PAIR, (pair + 1) * PAIR)
     for g in range(PASSES):
         bank = banks.tile([P, WORDS, PAIR], F32)
         for t in range(2):
             for u in range(WORDS):
-                if split is None:
-                    every_second = slice(WORDS * P * g + u, WORDS * P * (g + 1), WORDS)
-                    words = raw[:, 2 * pair + t, :].bitcast(F32)[:, every_second]
-                else:
-                    first = (WORDS * g + u) * P
-                    words = split[:, 2 * pair + t, first : first + P]
-                nc.tensor.transpose(bank[:, u, t * P : (t + 1) * P], words, ident[:])
+                first = (WORDS * g + u) * P
+                nc.tensor.transpose(
+                    bank[:, u, t * P : (t + 1) * P],
+                    split[:, 2 * pair + t, first : first + P],
+                    ident[:],
+                )
         hold_clock()
         nc.scalar.copy(out=grouped[:, g, cols, :], in_=bank[:].rearrange("p u r -> p r u"))
+
+
+def quantize_pair(nc, operand, pair):
+    grouped, codes, scales = operand[2], operand[3], operand[4]
+    cols = slice(pair * PAIR, (pair + 1) * PAIR)
     for g in range(PASSES):
         nc.vector.quantize_mx(
             out=codes[:, g, cols].bitcast(FP8X4),
@@ -109,13 +115,8 @@ def tile_constrainnet_kernel(tc, A, B, x0, net_input, T, out):
         def nothing():
             return None
 
-        def prepare_ab(pair, split, hold_clock):
-            prepare_pair(
-                nc, banks, ident, ab_raw, split, pair, ab_grouped, ab_codes, ab_scales, hold_clock
-            )
-
-        def prepare_v(pair, split, hold_clock):
-            prepare_pair(nc, banks, ident, v_raw, split, pair, v_grouped, v_codes, v_scales, hold_clock)
+        ab = (ab_raw, ab_split, ab_grouped, ab_codes, ab_scales)
+        v = (v_raw, v_split, v_grouped, v_codes, v_scales)
 
         def multiply(pair, h):
             n_cols = slice(h * N_HALF, (h + 1) * N_HALF)
@@ -155,8 +156,17 @@ def tile_constrainnet_kernel(tc, A, B, x0, net_input, T, out):
 
             for i in range(WARM_UP):
                 matmul_of_zeros()
-            prepare_ab(0, None, matmul_of_zeros)
-            prepare_ab(1, None, matmul_of_zeros)
+            split_words(nc, ab, 0)
+            transpose_pair(nc, banks, ident, ab, 0, matmul_of_zeros)
+            split_words(nc, ab, 1)
+            quantize_pair(nc, ab, 0)
+            transpose_pair(nc, banks, ident, ab, 1, matmul_of_zeros)
+            split_words(nc, v, 0)
+            quantize_pair(nc, ab, 1)
+            transpose_pair(nc, banks, ident, v, 0, matmul_of_zeros)
+            split_words(nc, v, 1)
+            quantize_pair(nc, v, 0)
+            transpose_pair(nc, banks, ident, v, 1, matmul_of_zeros)
 
             nc.vector.tensor_tensor(
                 out=r_first[:], in0=x_first[:], in1=x_given[:], op=mybir.AluOpType.subtract
@@ -165,19 +175,22 @@ def tile_constrainnet_kernel(tc, A, B, x0, net_input, T, out):
                 out=out[0:N_STATE].rearrange("(p c) -> p c", p=FIRST_P), in_=r_first[:]
             )
 
-            prepare_v(0, None, matmul_of_zeros)
-            prepare_v(1, None, matmul_of_zeros)
-            split_words(nc, v_raw, 2, v_split)
+            split_words(nc, v, 2)
+            quantize_pair(nc, v, 1)
+            split_words(nc, v, 3)
             multiply(0, 0)
-            prepare_v(2, v_split, nothing)
-            split_words(nc, v_raw, 3, v_split)
+            transpose_pair(nc, banks, ident, v, 2, nothing)
+            split_words(nc, ab, 2)
+            quantize_pair(nc, v, 2)
             multiply(1, 0)
-            prepare_v(3, v_split, nothing)
-            split_words(nc, ab_raw, 2, ab_split)
-            split_words(nc, ab_raw, 3, ab_split)
+            transpose_pair(nc, banks, ident, v, 3, nothing)
+            split_words(nc, ab, 3)
+            quantize_pair(nc, v, 3)
             multiply(2, 0)
-            prepare_ab(2, ab_split, nothing)
-            prepare_ab(3, ab_split, nothing)
+            transpose_pair(nc, banks, ident, ab, 2, nothing)
+            transpose_pair(nc, banks, ident, ab, 3, nothing)
+            quantize_pair(nc, ab, 2)
+            quantize_pair(nc, ab, 3)
             multiply(3, 0)
             for pair in range(SLOTS // 2):
                 multiply(pair, 1)

@@ -21,7 +21,6 @@ PAIR = 2 * P
 N_HALF = 512
 HALVES = N_STATE // N_HALF
 FIRST_P = 16
-WARM_UP = 4
 
 FLOPS = 2 * STEPS * N_STATE * N_ALL
 
@@ -35,20 +34,20 @@ def split_words(nc, operand, pair):
         )
 
 
-def transpose_pair(nc, banks, ident, operand, pair, hold_clock):
-    split, grouped = operand[1], operand[2]
+def transpose_pair(nc, banks, ident, operand, pair, sorted_words):
+    raw, split, grouped = operand[0], operand[1], operand[2]
     cols = slice(pair * PAIR, (pair + 1) * PAIR)
     for g in range(PASSES):
         bank = banks.tile([P, WORDS, PAIR], F32)
         for t in range(2):
             for u in range(WORDS):
-                first = (WORDS * g + u) * P
-                nc.tensor.transpose(
-                    bank[:, u, t * P : (t + 1) * P],
-                    split[:, 2 * pair + t, first : first + P],
-                    ident[:],
-                )
-        hold_clock()
+                if sorted_words:
+                    first = (WORDS * g + u) * P
+                    words = split[:, 2 * pair + t, first : first + P]
+                else:
+                    every_second = slice(WORDS * P * g + u, WORDS * P * (g + 1), WORDS)
+                    words = raw[:, 2 * pair + t, 0:N_ALL].bitcast(F32)[:, every_second]
+                nc.tensor.transpose(bank[:, u, t * P : (t + 1) * P], words, ident[:])
         nc.scalar.copy(out=grouped[:, g, cols, :], in_=bank[:].rearrange("p u r -> p r u"))
 
 
@@ -105,16 +104,6 @@ def tile_constrainnet_kernel(tc, A, B, x0, net_input, T, out):
             slots = slice(2 * pair, 2 * pair + 2)
             nc.sync.dma_start(out=v_raw[:, slots, :], in_=v_rows[:, slots, :])
 
-        zeros = keep.tile([P, N_HALF], BF16)
-        nc.vector.memset(zeros[:], 0.0)
-
-        def matmul_of_zeros():
-            unread = sums.tile([P, N_HALF], F32, tag="acc")
-            nc.tensor.matmul(out=unread[:], lhsT=zeros[:, 0:P], rhs=zeros[:], start=True, stop=True)
-
-        def nothing():
-            return None
-
         ab = (ab_raw, ab_split, ab_grouped, ab_codes, ab_scales)
         v = (v_raw, v_split, v_grouped, v_codes, v_scales)
 
@@ -154,19 +143,13 @@ def tile_constrainnet_kernel(tc, A, B, x0, net_input, T, out):
             load_ab(2)
             load_ab(3)
 
-            for i in range(WARM_UP):
-                matmul_of_zeros()
-            split_words(nc, ab, 0)
-            transpose_pair(nc, banks, ident, ab, 0, matmul_of_zeros)
-            split_words(nc, ab, 1)
+            transpose_pair(nc, banks, ident, ab, 0, False)
             quantize_pair(nc, ab, 0)
-            transpose_pair(nc, banks, ident, ab, 1, matmul_of_zeros)
-            split_words(nc, v, 0)
+            transpose_pair(nc, banks, ident, ab, 1, False)
             quantize_pair(nc, ab, 1)
-            transpose_pair(nc, banks, ident, v, 0, matmul_of_zeros)
-            split_words(nc, v, 1)
+            transpose_pair(nc, banks, ident, v, 0, False)
             quantize_pair(nc, v, 0)
-            transpose_pair(nc, banks, ident, v, 1, matmul_of_zeros)
+            transpose_pair(nc, banks, ident, v, 1, False)
 
             nc.vector.tensor_tensor(
                 out=r_first[:], in0=x_first[:], in1=x_given[:], op=mybir.AluOpType.subtract
@@ -179,16 +162,16 @@ def tile_constrainnet_kernel(tc, A, B, x0, net_input, T, out):
             quantize_pair(nc, v, 1)
             split_words(nc, v, 3)
             multiply(0, 0)
-            transpose_pair(nc, banks, ident, v, 2, nothing)
+            transpose_pair(nc, banks, ident, v, 2, True)
             split_words(nc, ab, 2)
             quantize_pair(nc, v, 2)
             multiply(1, 0)
-            transpose_pair(nc, banks, ident, v, 3, nothing)
+            transpose_pair(nc, banks, ident, v, 3, True)
             split_words(nc, ab, 3)
             quantize_pair(nc, v, 3)
             multiply(2, 0)
-            transpose_pair(nc, banks, ident, ab, 2, nothing)
-            transpose_pair(nc, banks, ident, ab, 3, nothing)
+            transpose_pair(nc, banks, ident, ab, 2, True)
+            transpose_pair(nc, banks, ident, ab, 3, True)
             quantize_pair(nc, ab, 2)
             quantize_pair(nc, ab, 3)
             multiply(3, 0)

@@ -107,28 +107,38 @@ def tile_constrainnet_kernel(tc, A, B, x0, net_input, T, out):
         ab = (ab_raw, ab_split, ab_grouped, ab_codes, ab_scales)
         v = (v_raw, v_split, v_grouped, v_codes, v_scales)
 
-        def multiply(pair, h):
-            n_cols = slice(h * N_HALF, (h + 1) * N_HALF)
-            for s in range(2 * pair, 2 * pair + 2):
-                m_cols = slice(s * P, (s + 1) * P)
-                acc = sums.tile([P, N_HALF], F32)
-                for g in range(PASSES):
-                    nc.tensor.matmul_mx(
-                        out=acc[:],
-                        lhsT=v_codes[:, g, m_cols].bitcast(FP8X4),
-                        lhsT_scale=v_scales[:, g, m_cols],
-                        rhs=ab_codes[:, g, n_cols].bitcast(FP8X4),
-                        rhs_scale=ab_scales[:, g, n_cols],
-                        start=(g == 0),
-                        stop=(g == PASSES - 1),
-                    )
-                nc.vector.tensor_tensor(
-                    out=r_sb[:, s, n_cols],
-                    in0=acc[:],
-                    in1=v_raw[:, s + 1, n_cols],
-                    op=mybir.AluOpType.subtract,
+        open_sums = {}
+
+        def product(s, first, width=N_HALF):
+            n_cols = slice(first, first + width)
+            m_cols = slice(s * P, (s + 1) * P)
+            acc = sums.tile([P, N_HALF], F32)
+            for g in range(PASSES):
+                nc.tensor.matmul_mx(
+                    out=acc[:, 0:width],
+                    lhsT=v_codes[:, g, m_cols].bitcast(FP8X4),
+                    lhsT_scale=v_scales[:, g, m_cols],
+                    rhs=ab_codes[:, g, n_cols].bitcast(FP8X4),
+                    rhs_scale=ab_scales[:, g, n_cols],
+                    start=(g == 0),
+                    stop=(g == PASSES - 1),
                 )
-                nc.sync.dma_start(out=r_next[:, s, n_cols], in_=r_sb[:, s, n_cols])
+            open_sums[(s, first)] = acc
+
+        def residual(s, first, width=N_HALF):
+            n_cols = slice(first, first + width)
+            nc.vector.tensor_tensor(
+                out=r_sb[:, s, n_cols],
+                in0=open_sums[(s, first)][:, 0:width],
+                in1=v_raw[:, s + 1, n_cols],
+                op=mybir.AluOpType.subtract,
+            )
+            nc.sync.dma_start(out=r_next[:, s, n_cols], in_=r_sb[:, s, n_cols])
+
+        def finish(slots, first, width=N_HALF):
+            for s in slots:
+                product(s, first, width)
+                residual(s, first, width)
 
         with tc.manual_schedule():
             nc.scalar.dma_start(
@@ -137,11 +147,13 @@ def tile_constrainnet_kernel(tc, A, B, x0, net_input, T, out):
             nc.scalar.dma_start(out=x_given[:], in_=x0.rearrange("(p c) -> p c", p=FIRST_P))
             load_ab(0)
             load_ab(1)
-            for pair in range(SLOTS // 2):
-                load_v(pair)
-            nc.sync.dma_start(out=v_raw[:, SLOTS, 0:N_STATE], in_=v_next[:, SLOTS - 1, 0:N_STATE])
+            load_v(0)
+            load_v(1)
+            load_v(2)
             load_ab(2)
             load_ab(3)
+            load_v(3)
+            nc.sync.dma_start(out=v_raw[:, SLOTS, 0:N_STATE], in_=v_next[:, SLOTS - 1, 0:N_STATE])
 
             transpose_pair(nc, banks, ident, ab, 0, False)
             quantize_pair(nc, ab, 0)
@@ -160,20 +172,30 @@ def tile_constrainnet_kernel(tc, A, B, x0, net_input, T, out):
 
             split_words(nc, v, 2)
             quantize_pair(nc, v, 1)
-            split_words(nc, v, 3)
-            multiply(0, 0)
-            transpose_pair(nc, banks, ident, v, 2, True)
             split_words(nc, ab, 2)
-            quantize_pair(nc, v, 2)
-            multiply(1, 0)
-            transpose_pair(nc, banks, ident, v, 3, True)
+            finish((0, 1), 0)
+            transpose_pair(nc, banks, ident, v, 2, True)
             split_words(nc, ab, 3)
-            quantize_pair(nc, v, 3)
-            multiply(2, 0)
+            product(2, 0)
+            quantize_pair(nc, v, 2)
             transpose_pair(nc, banks, ident, ab, 2, True)
-            transpose_pair(nc, banks, ident, ab, 3, True)
+            product(3, 0)
+            residual(2, 0)
+            split_words(nc, v, 3)
             quantize_pair(nc, ab, 2)
+            transpose_pair(nc, banks, ident, ab, 3, True)
+            residual(3, 0)
+            product(4, 0)
+            transpose_pair(nc, banks, ident, v, 3, True)
             quantize_pair(nc, ab, 3)
-            multiply(3, 0)
-            for pair in range(SLOTS // 2):
-                multiply(pair, 1)
+            residual(4, 0)
+            product(5, 0)
+            product(0, N_HALF)
+            residual(5, 0)
+            residual(0, N_HALF)
+            quantize_pair(nc, v, 3)
+            finish(range(1, 6), N_HALF)
+            finish((6, 7), 0)
+            finish((6,), N_HALF)
+            finish((7,), N_HALF, N_HALF // 2)
+            finish((7,), N_HALF + N_HALF // 2, N_HALF // 2)

@@ -34,12 +34,15 @@ def split_words(nc, operand, pair):
         )
 
 
-def transpose_pair(nc, banks, ident, operand, pair, sorted_words):
+BY_PASS = (((0, 0), (1, 0)), ((0, 1), (1, 1)), ((0, 2), (1, 2)))
+BY_TILE = (((0, 0), (0, 1)), ((1, 0), (1, 1)), ((0, 2), (1, 2)))
+
+
+def transpose_pair(nc, banks, ident, operand, pair, contents, sorted_words, shared=False):
     raw, split, grouped = operand[0], operand[1], operand[2]
-    cols = slice(pair * PAIR, (pair + 1) * PAIR)
-    for g in range(PASSES):
-        bank = banks.tile([P, WORDS, PAIR], F32)
-        for t in range(2):
+    for content in contents:
+        bank = banks.tile([P, 2, WORDS, P], F32)
+        for x, (t, g) in enumerate(content):
             for u in range(WORDS):
                 if sorted_words:
                     first = (WORDS * g + u) * P
@@ -47,8 +50,17 @@ def transpose_pair(nc, banks, ident, operand, pair, sorted_words):
                 else:
                     every_second = slice(WORDS * P * g + u, WORDS * P * (g + 1), WORDS)
                     words = raw[:, 2 * pair + t, 0:N_ALL].bitcast(F32)[:, every_second]
-                nc.tensor.transpose(bank[:, u, t * P : (t + 1) * P], words, ident[:])
-        nc.scalar.copy(out=grouped[:, g, cols, :], in_=bank[:].rearrange("p u r -> p r u"))
+                nc.tensor.transpose(bank[:, x, u, :], words, ident[:])
+        t, g = content[0]
+        if content[1][1] == g:
+            out = grouped[:, pair, g, :, :].rearrange("p (t r) u -> p t r u", t=2)
+        else:
+            out = grouped[:, pair, g : g + 2, t * P : (t + 1) * P, :]
+        in_order = bank[:].rearrange("p x u r -> p x r u")
+        if shared and content == contents[1]:
+            nc.vector.tensor_copy(out=out, in_=in_order)
+        else:
+            nc.scalar.copy(out=out, in_=in_order)
 
 
 def quantize_pair(nc, operand, pair):
@@ -58,7 +70,7 @@ def quantize_pair(nc, operand, pair):
         nc.vector.quantize_mx(
             out=codes[:, g, cols].bitcast(FP8X4),
             scales=scales[:, g, cols],
-            in_=grouped[:, g, cols, :].rearrange("p r u -> p (r u)").bitcast(BF16),
+            in_=grouped[:, pair, g, :, :].rearrange("p r u -> p (r u)").bitcast(BF16),
         )
 
 
@@ -84,8 +96,8 @@ def tile_constrainnet_kernel(tc, A, B, x0, net_input, T, out):
         v_raw = keep.tile([P, SLOTS + 1, N_ALL], BF16)
         ab_split = keep.tile([P, TILES, N_ALL // 2], F32)
         v_split = keep.tile([P, SLOTS, N_ALL // 2], F32)
-        ab_grouped = keep.tile([P, PASSES, N_STATE, WORDS], F32, align_bytes=64)
-        v_grouped = keep.tile([P, PASSES, STEPS, WORDS], F32, align_bytes=64)
+        ab_grouped = keep.tile([P, TILES // 2, PASSES, PAIR, WORDS], F32, align_bytes=64)
+        v_grouped = keep.tile([P, SLOTS // 2, PASSES, PAIR, WORDS], F32, align_bytes=64)
         ab_codes = keep.tile([P, PASSES, N_STATE], U32, align_bytes=64)
         ab_scales = keep.tile([P, PASSES, N_STATE], U8, align_bytes=64)
         v_codes = keep.tile([P, PASSES, STEPS], U32, align_bytes=64)
@@ -141,52 +153,47 @@ def tile_constrainnet_kernel(tc, A, B, x0, net_input, T, out):
                 residual(s, first, width)
 
         with tc.manual_schedule():
-            nc.scalar.dma_start(
-                out=x_first[:], in_=net_input[0:N_STATE].rearrange("(p c) -> p c", p=FIRST_P)
-            )
-            nc.scalar.dma_start(out=x_given[:], in_=x0.rearrange("(p c) -> p c", p=FIRST_P))
-            load_ab(0)
+            for m in (0, 1):
+                nc.sync.dma_start(out=ab_raw[:, m, 0:N_STATE], in_=a_rows[:, m, :])
+            nc.sync.dma_start(out=ab_raw[:, 0:2, N_STATE:N_ALL], in_=b_rows[:, 0:2, :])
             load_ab(1)
-            load_v(0)
-            load_v(1)
+            for s in (0, 1, 2, 3):
+                nc.sync.dma_start(out=v_raw[:, s, :], in_=v_rows[:, s, :])
             load_v(2)
             load_ab(2)
             load_ab(3)
             load_v(3)
+            nc.sync.dma_start(
+                out=x_first[:], in_=net_input[0:N_STATE].rearrange("(p c) -> p c", p=FIRST_P)
+            )
+            nc.sync.dma_start(out=x_given[:], in_=x0.rearrange("(p c) -> p c", p=FIRST_P))
             nc.sync.dma_start(out=v_raw[:, SLOTS, 0:N_STATE], in_=v_next[:, SLOTS - 1, 0:N_STATE])
 
-            transpose_pair(nc, banks, ident, ab, 0, False)
+            transpose_pair(nc, banks, ident, ab, 0, BY_TILE, False)
             quantize_pair(nc, ab, 0)
-            transpose_pair(nc, banks, ident, ab, 1, False)
+            transpose_pair(nc, banks, ident, ab, 1, BY_TILE, False, shared=True)
             quantize_pair(nc, ab, 1)
-            transpose_pair(nc, banks, ident, v, 0, False)
+            transpose_pair(nc, banks, ident, v, 0, BY_TILE, False, shared=True)
             quantize_pair(nc, v, 0)
-            transpose_pair(nc, banks, ident, v, 1, False)
-
-            nc.vector.tensor_tensor(
-                out=r_first[:], in0=x_first[:], in1=x_given[:], op=mybir.AluOpType.subtract
-            )
-            nc.sync.dma_start(
-                out=out[0:N_STATE].rearrange("(p c) -> p c", p=FIRST_P), in_=r_first[:]
-            )
+            transpose_pair(nc, banks, ident, v, 1, BY_TILE, False)
 
             split_words(nc, v, 2)
             quantize_pair(nc, v, 1)
             split_words(nc, ab, 2)
             finish((0, 1), 0)
-            transpose_pair(nc, banks, ident, v, 2, True)
+            transpose_pair(nc, banks, ident, v, 2, BY_PASS, True)
             split_words(nc, ab, 3)
             product(2, 0)
             quantize_pair(nc, v, 2)
-            transpose_pair(nc, banks, ident, ab, 2, True)
+            transpose_pair(nc, banks, ident, ab, 2, BY_PASS, True)
             product(3, 0)
             residual(2, 0)
             split_words(nc, v, 3)
             quantize_pair(nc, ab, 2)
-            transpose_pair(nc, banks, ident, ab, 3, True)
+            transpose_pair(nc, banks, ident, ab, 3, BY_PASS, True)
             residual(3, 0)
             product(4, 0)
-            transpose_pair(nc, banks, ident, v, 3, True)
+            transpose_pair(nc, banks, ident, v, 3, BY_PASS, True)
             quantize_pair(nc, ab, 3)
             residual(4, 0)
             product(5, 0)
@@ -194,6 +201,12 @@ def tile_constrainnet_kernel(tc, A, B, x0, net_input, T, out):
             residual(5, 0)
             residual(0, N_HALF)
             quantize_pair(nc, v, 3)
+            nc.vector.tensor_tensor(
+                out=r_first[:], in0=x_first[:], in1=x_given[:], op=mybir.AluOpType.subtract
+            )
+            nc.sync.dma_start(
+                out=out[0:N_STATE].rearrange("(p c) -> p c", p=FIRST_P), in_=r_first[:]
+            )
             finish(range(1, 6), N_HALF)
             finish((6, 7), 0)
             finish((6,), N_HALF)

@@ -41,7 +41,7 @@ BY_TILE = (((0, 0), (0, 1)), ((1, 0), (1, 1)), ((0, 2), (1, 2)))
 def transpose_pair(nc, banks, ident, operand, pair, contents, sorted_words, shared=False):
     raw, split, grouped = operand[0], operand[1], operand[2]
     for content in contents:
-        bank = banks.tile([P, 2, WORDS, P], F32)
+        bank = banks.tile([P, WORDS, 2, P], F32)
         for x, (t, g) in enumerate(content):
             for u in range(WORDS):
                 if sorted_words:
@@ -50,17 +50,20 @@ def transpose_pair(nc, banks, ident, operand, pair, contents, sorted_words, shar
                 else:
                     every_second = slice(WORDS * P * g + u, WORDS * P * (g + 1), WORDS)
                     words = raw[:, 2 * pair + t, 0:N_ALL].bitcast(F32)[:, every_second]
-                nc.tensor.transpose(bank[:, x, u, :], words, ident[:])
+                nc.tensor.transpose(bank[:, u, x, :], words, ident[:])
         t, g = content[0]
         if content[1][1] == g:
-            out = grouped[:, pair, g, :, :].rearrange("p (t r) u -> p t r u", t=2)
+            out = grouped[:, pair, g, :, :].rearrange("p (c i) u -> p c u i", i=2)
+            in_pairs = bank[:].rearrange("p u x r -> p u (x r)").rearrange("p u (c i) -> p c u i", i=2)
         else:
-            out = grouped[:, pair, g : g + 2, t * P : (t + 1) * P, :]
-        in_order = bank[:].rearrange("p x u r -> p x r u")
+            out = grouped[:, pair, g : g + 2, t * P : (t + 1) * P, :].rearrange(
+                "p x (c i) u -> p x c u i", i=2
+            )
+            in_pairs = bank[:].rearrange("p u x (c i) -> p x c u i", i=2)
         if shared and content == contents[1]:
-            nc.vector.tensor_copy(out=out, in_=in_order)
+            nc.vector.tensor_copy(out=out, in_=in_pairs)
         else:
-            nc.scalar.copy(out=out, in_=in_order)
+            nc.scalar.copy(out=out, in_=in_pairs)
 
 
 def quantize_pair(nc, operand, pair):

from contextlib import ExitStack

import concourse.mybir as mybir
from concourse.masks import make_identity

F32 = mybir.dt.float32
BF16 = mybir.dt.bfloat16
U32 = mybir.dt.uint32
U8 = mybir.dt.uint8
FP8X4 = mybir.dt.float8_e4m3fn_x4

P = 128
N_STATE = 1024
N_ALL = 1536
STEPS = 1024
PASSES = 3
WORDS = 2
SLOTS = STEPS // P
TILES = N_STATE // P
PAIR = 2 * P
N_HALF = 512
HALVES = N_STATE // N_HALF
FIRST_P = 16

FLOPS = 2 * STEPS * N_STATE * N_ALL


def split_words(nc, operand, pair):
    raw, split = operand[0], operand[1]
    for t in (2 * pair, 2 * pair + 1):
        nc.vector.tensor_copy(
            out=split[:, t, :].rearrange("p (g u w) -> p u g w", u=WORDS, w=P),
            in_=raw[:, t, 0:N_ALL].bitcast(F32).rearrange("p (g w u) -> p u g w", u=WORDS, w=P),
        )


BY_PASS = (((0, 0), (1, 0)), ((0, 1), (1, 1)), ((0, 2), (1, 2)))
BY_TILE = (((0, 0), (0, 1)), ((1, 0), (1, 1)), ((0, 2), (1, 2)))


def transpose_pair(nc, banks, ident, operand, pair, contents, sorted_words, shared=False):
    raw, split, grouped = operand[0], operand[1], operand[2]
    for content in contents:
        bank = banks.tile([P, WORDS, 2, P], F32)
        for x, (t, g) in enumerate(content):
            for u in range(WORDS):
                if sorted_words:
                    first = (WORDS * g + u) * P
                    words = split[:, 2 * pair + t, first : first + P]
                else:
                    every_second = slice(WORDS * P * g + u, WORDS * P * (g + 1), WORDS)
                    words = raw[:, 2 * pair + t, 0:N_ALL].bitcast(F32)[:, every_second]
                nc.tensor.transpose(bank[:, u, x, :], words, ident[:])
        t, g = content[0]
        if content[1][1] == g:
            out = grouped[:, pair, g, :, :].rearrange("p (c i) u -> p c u i", i=2)
            in_pairs = bank[:].rearrange("p u x r -> p u (x r)").rearrange("p u (c i) -> p c u i", i=2)
        else:
            out = grouped[:, pair, g : g + 2, t * P : (t + 1) * P, :].rearrange(
                "p x (c i) u -> p x c u i", i=2
            )
            in_pairs = bank[:].rearrange("p u x (c i) -> p x c u i", i=2)
        if shared and content == contents[1]:
            nc.vector.tensor_copy(out=out, in_=in_pairs)
        else:
            nc.scalar.copy(out=out, in_=in_pairs)


def quantize_pair(nc, operand, pair):
    grouped, codes, scales = operand[2], operand[3], operand[4]
    cols = slice(pair * PAIR, (pair + 1) * PAIR)
    for g in range(PASSES):
        nc.vector.quantize_mx(
            out=codes[:, g, cols].bitcast(FP8X4),
            scales=scales[:, g, cols],
            in_=grouped[:, pair, g, :, :].rearrange("p r u -> p (r u)").bitcast(BF16),
        )


def tile_constrainnet_kernel(tc, A, B, x0, net_input, T, out):
    nc = tc.nc
    assert T == STEPS + 1

    v_rows = net_input[0 : STEPS * N_ALL].rearrange("(p s k) -> p s k", s=SLOTS, k=N_ALL)
    v_next = net_input[N_ALL : (STEPS + 1) * N_ALL].rearrange("(p s k) -> p s k", s=SLOTS, k=N_ALL)
    r_next = out[N_STATE : (STEPS + 1) * N_STATE].rearrange("(p s i) -> p s i", s=SLOTS, i=N_STATE)
    a_rows = A.rearrange("(m p) k -> p m k", p=P)
    b_rows = B.rearrange("(m p) k -> p m k", p=P)

    with ExitStack() as ctx:
        keep = ctx.enter_context(tc.tile_pool(name="keep", bufs=1))
        banks = ctx.enter_context(tc.psum_pool(name="banks", bufs=4))
        sums = ctx.enter_context(tc.psum_pool(name="sums", bufs=4))

        ident = keep.tile([P, P], F32)
        make_identity(nc, ident[:])

        ab_raw = keep.tile([P, TILES, N_ALL], BF16)
        v_raw = keep.tile([P, SLOTS + 1, N_ALL], BF16)
        ab_split = keep.tile([P, TILES, N_ALL // 2], F32)
        v_split = keep.tile([P, SLOTS, N_ALL // 2], F32)
        ab_grouped = keep.tile([P, TILES // 2, PASSES, PAIR, WORDS], F32, align_bytes=64)
        v_grouped = keep.tile([P, SLOTS // 2, PASSES, PAIR, WORDS], F32, align_bytes=64)
        ab_codes = keep.tile([P, PASSES, N_STATE], U32, align_bytes=64)
        ab_scales = keep.tile([P, PASSES, N_STATE], U8, align_bytes=64)
        v_codes = keep.tile([P, PASSES, STEPS], U32, align_bytes=64)
        v_scales = keep.tile([P, PASSES, STEPS], U8, align_bytes=64)
        r_sb = keep.tile([P, SLOTS, N_STATE], F32)
        x_first = keep.tile([FIRST_P, N_STATE // FIRST_P], BF16)
        x_given = keep.tile([FIRST_P, N_STATE // FIRST_P], BF16)
        r_first = keep.tile([FIRST_P, N_STATE // FIRST_P], F32)

        def load_ab(pair):
            tiles = slice(2 * pair, 2 * pair + 2)
            nc.sync.dma_start(out=ab_raw[:, tiles, 0:N_STATE], in_=a_rows[:, tiles, :])
            nc.sync.dma_start(out=ab_raw[:, tiles, N_STATE:N_ALL], in_=b_rows[:, tiles, :])

        def load_v(pair):
            slots = slice(2 * pair, 2 * pair + 2)
            nc.sync.dma_start(out=v_raw[:, slots, :], in_=v_rows[:, slots, :])

        ab = (ab_raw, ab_split, ab_grouped, ab_codes, ab_scales)
        v = (v_raw, v_split, v_grouped, v_codes, v_scales)

        open_sums = {}

        def product(s, first, width=N_HALF):
            n_cols = slice(first, first + width)
            m_cols = slice(s * P, (s + 1) * P)
            acc = sums.tile([P, N_HALF], F32)
            for g in range(PASSES):
                nc.tensor.matmul_mx(
                    out=acc[:, 0:width],
                    lhsT=v_codes[:, g, m_cols].bitcast(FP8X4),
                    lhsT_scale=v_scales[:, g, m_cols],
                    rhs=ab_codes[:, g, n_cols].bitcast(FP8X4),
                    rhs_scale=ab_scales[:, g, n_cols],
                    start=(g == 0),
                    stop=(g == PASSES - 1),
                )
            open_sums[(s, first)] = acc

        def residual(s, first, width=N_HALF):
            n_cols = slice(first, first + width)
            nc.vector.tensor_tensor(
                out=r_sb[:, s, n_cols],
                in0=open_sums[(s, first)][:, 0:width],
                in1=v_raw[:, s + 1, n_cols],
                op=mybir.AluOpType.subtract,
            )
            nc.sync.dma_start(out=r_next[:, s, n_cols], in_=r_sb[:, s, n_cols])

        def finish(slots, first, width=N_HALF):
            for s in slots:
                product(s, first, width)
                residual(s, first, width)

        with tc.manual_schedule():
            for m in (0, 1):
                nc.sync.dma_start(out=ab_raw[:, m, 0:N_STATE], in_=a_rows[:, m, :])
            nc.sync.dma_start(out=ab_raw[:, 0:2, N_STATE:N_ALL], in_=b_rows[:, 0:2, :])
            load_ab(1)
            for s in (0, 1, 2, 3):
                nc.sync.dma_start(out=v_raw[:, s, :], in_=v_rows[:, s, :])
            load_v(2)
            load_ab(2)
            load_ab(3)
            load_v(3)
            nc.sync.dma_start(
                out=x_first[:], in_=net_input[0:N_STATE].rearrange("(p c) -> p c", p=FIRST_P)
            )
            nc.sync.dma_start(out=x_given[:], in_=x0.rearrange("(p c) -> p c", p=FIRST_P))
            nc.sync.dma_start(out=v_raw[:, SLOTS, 0:N_STATE], in_=v_next[:, SLOTS - 1, 0:N_STATE])

            transpose_pair(nc, banks, ident, ab, 0, BY_TILE, False)
            quantize_pair(nc, ab, 0)
            transpose_pair(nc, banks, ident, ab, 1, BY_TILE, False, shared=True)
            quantize_pair(nc, ab, 1)
            transpose_pair(nc, banks, ident, v, 0, BY_TILE, False, shared=True)
            quantize_pair(nc, v, 0)
            transpose_pair(nc, banks, ident, v, 1, BY_TILE, False)

            split_words(nc, v, 2)
            quantize_pair(nc, v, 1)
            split_words(nc, ab, 2)
            finish((0, 1), 0)
            transpose_pair(nc, banks, ident, v, 2, BY_PASS, True)
            split_words(nc, ab, 3)
            product(2, 0)
            quantize_pair(nc, v, 2)
            transpose_pair(nc, banks, ident, ab, 2, BY_PASS, True)
            product(3, 0)
            residual(2, 0)
            split_words(nc, v, 3)
            quantize_pair(nc, ab, 2)
            transpose_pair(nc, banks, ident, ab, 3, BY_PASS, True)
            residual(3, 0)
            product(4, 0)
            transpose_pair(nc, banks, ident, v, 3, BY_PASS, True)
            quantize_pair(nc, ab, 3)
            residual(4, 0)
            product(5, 0)
            product(0, N_HALF)
            residual(5, 0)
            residual(0, N_HALF)
            quantize_pair(nc, v, 3)
            nc.vector.tensor_tensor(
                out=r_first[:], in0=x_first[:], in1=x_given[:], op=mybir.AluOpType.subtract
            )
            nc.sync.dma_start(
                out=out[0:N_STATE].rearrange("(p c) -> p c", p=FIRST_P), in_=r_first[:]
            )
            finish(range(1, 6), N_HALF)
            finish((6, 7), 0)
            finish((6,), N_HALF)
            finish((7,), N_HALF, N_HALF // 2)
            finish((7,), N_HALF + N_HALF // 2, N_HALF // 2)
